import numpy as np
import ml_dtypes

BF16 = ml_dtypes.bfloat16


def bf(x):
    return np.asarray(x, np.float32).astype(BF16)


def f32(x):
    return np.asarray(x, np.float32)


def f64(x):
    return np.asarray(x).astype(np.float64)


def striped(idx):
    return np.tile(idx.reshape(-1, 16).T, (8, 1))


D, V, B, T, H, N = 512, 4096, 4, 512, 4, 2048
HD = D // H


def setup_inputs():
    r = np.random.standard_normal
    return {
        'tok_emb': f32(r((D, V))),
        'pos_emb': f32(0.5 * r((D, T))),
        'type_emb': f32(0.5 * r((D, 1))),
        'wq': bf(r((D, D)) / np.sqrt(D)),
        'bq': f32(0.1 * r((D, 1))),
        'wk': bf(r((D, D)) / np.sqrt(D)),
        'wv': bf(2.0 * r((D, D)) / np.sqrt(D)),
        'bv': f32(0.1 * r((D, 1))),
        'wo': bf(2.0 * r((D, D)) / np.sqrt(D)),
        'bo': f32(0.1 * r((D, 1))),
        'offs': striped(np.random.permutation(np.tile(np.arange(V), 2))[:N]),
    }


def reference(tok_emb, pos_emb, type_emb, wq, bq, wk, wv, bv, wo, bo, offs):
    idx = offs[:16].T.reshape(-1)
    x = f64(tok_emb)[:, idx] + np.tile(f64(pos_emb), (1, B)) + f64(type_emb)
    q = (f64(wq).T @ x + f64(bq)).reshape(H, HD, B, T)
    k = (f64(wk).T @ x).reshape(H, HD, B, T)
    v = (f64(wv).T @ x + f64(bv)).reshape(H, HD, B, T)
    s = np.einsum('hebt,hebu->hbtu', q, k) / np.sqrt(HD)
    p = np.exp(s - s.max(axis=-1, keepdims=True))
    a = p / p.sum(axis=-1, keepdims=True)
    o = np.einsum('hbtu,hebu->hebt', a, v).reshape(D, N)
    return x + f64(wo).T @ o + f64(bo)

@@ -1,0 +1,170 @@
+import math
+
+import concourse.mybir as mybir
+from concourse.masks import make_identity
+
+F32, BF16, U16 = mybir.dt.float32, mybir.dt.bfloat16, mybir.dt.uint16
+ADD = mybir.AluOpType.add
+FUNC = mybir.ActivationFunctionType
+ALONG_FREE = mybir.AxisListType.X
+
+P = 128
+D = 512
+V = 4096
+B = 4
+T = 512
+H = 4
+CB = D // P
+TB = T // P
+PER_COLUMN = 16
+SCALE = 1.0 / math.sqrt(P)
+
+FLOPS = 4 * 2 * D * D * B * T + 2 * B * H * 2 * T * T * P
+
+
+def tile_enhancedtransformertextclassifier_b_kernel(
+    tc, tok_emb, pos_emb, type_emb, wq, bq, wk, wv, bv, wo, bo, offs, out
+):
+    nc = tc.nc
+    with (
+        tc.tile_pool(name="held", bufs=1) as held,
+        tc.tile_pool(name="sequence", bufs=2) as sequence,
+        tc.tile_pool(name="work", bufs=3) as work,
+        tc.tile_pool(name="stat", bufs=4) as stat,
+        tc.psum_pool(name="psum_acc", bufs=2) as psum_acc,
+        tc.psum_pool(name="psum_s", bufs=3) as psum_s,
+        tc.psum_pool(name="psum_t", bufs=2) as psum_t,
+        tc.psum_pool(name="psum_o", bufs=1) as psum_o,
+    ):
+        offsets = held.tile([P, B * T // PER_COLUMN], U16, name="offsets")
+        nc.sync.dma_start(offsets[:], offs)
+
+        tok = [held.tile([P, V], F32, name=f"tok{c}") for c in range(CB)]
+        for c in range(CB):
+            nc.sync.dma_start(tok[c][:], tok_emb[c * P : (c + 1) * P, :])
+
+        pos = held.tile([P, CB, T], F32, name="pos")
+        for c in range(CB):
+            nc.scalar.dma_start(pos[:, c, :], pos_emb[c * P : (c + 1) * P, :])
+        weights = {}
+        for name, w in (("q", wq), ("k", wk), ("v", wv), ("o", wo)):
+            weights[name] = held.tile([P, CB, D], BF16, name=f"w{name}")
+            nc.scalar.dma_start(weights[name][:], w.rearrange("(c p) m -> p c m", p=P))
+
+        bv_rows = held.tile([P, D], F32, name="bv_rows")
+        nc.gpsimd.dma_start(bv_rows[:], bv.rearrange("m o -> (m o)").partition_broadcast(P))
+
+        identity_f = held.tile([P, P], F32, name="identity_f")
+        make_identity(nc, identity_f[:])
+        identity_b = held.tile([P, P], BF16, name="identity_b")
+        make_identity(nc, identity_b[:])
+        rows = held.tile([P, P], F32, name="rows")
+        nc.vector.memset(rows[:], 0.0)
+        for n, vector in enumerate((type_emb, bq, bo)):
+            nc.gpsimd.dma_start(
+                rows[n * CB : (n + 1) * CB, :], vector.rearrange("(c p) o -> c (p o)", p=P)
+            )
+        acc = psum_acc.tile([P, T], F32, name="acc")
+        nc.tensor.transpose(acc[:, 0:P], rows[:], identity_f[:])
+        columns = held.tile([P, 3 * CB], F32, name="columns")
+        nc.vector.tensor_copy(columns[:], acc[:, 0 : 3 * CB])
+        type_col = [columns[:, c : c + 1] for c in range(CB)]
+        bq_col = [columns[:, CB + c : CB + c + 1] for c in range(CB)]
+        bo_col = [columns[:, 2 * CB + c : 2 * CB + c + 1] for c in range(CB)]
+
+        pos_type = held.tile([P, CB, T], F32, name="pos_type")
+        x = [held.tile([P, B * T], F32, name=f"x{c}") for c in range(CB)]
+        x_bf = [held.tile([P, B * T], BF16, name=f"x_bf{c}") for c in range(CB)]
+        for c in range(CB):
+            nc.vector.tensor_scalar_add(pos_type[:, c, :], pos[:, c, :], type_col[c])
+            for b in range(B):
+                seq = slice(b * T, (b + 1) * T)
+                piece = offsets[:, b * T // PER_COLUMN : (b + 1) * T // PER_COLUMN]
+                nc.vector.tensor_tensor(
+                    x[c][:, seq], tok[c][:].indirect(piece), pos_type[:, c, :], ADD
+                )
+                nc.gpsimd.tensor_copy(x_bf[c][:, seq], x[c][:, seq])
+
+        for b in range(B):
+            seq = slice(b * T, (b + 1) * T)
+
+            q = sequence.tile([P, H, T], BF16, name="q")
+            k = sequence.tile([P, H, T], BF16, name="k")
+            for h in range(H):
+                head = slice(h * P, (h + 1) * P)
+                acc = psum_acc.tile([P, T], F32, name="acc")
+                for c in range(CB):
+                    nc.tensor.matmul(
+                        acc[:], weights["q"][:, c, head], x_bf[c][:, seq],
+                        start=(c == 0), stop=(c == CB - 1),
+                    )
+                nc.scalar.activation(q[:, h, :], acc[:], FUNC.Identity, bias=bq_col[h])
+                acc = psum_acc.tile([P, T], F32, name="acc")
+                for c in range(CB):
+                    nc.tensor.matmul(
+                        acc[:], weights["k"][:, c, head], x_bf[c][:, seq],
+                        start=(c == 0), stop=(c == CB - 1),
+                    )
+                nc.scalar.copy(k[:, h, :], acc[:])
+
+            v_t = sequence.tile([P, TB, D], BF16, name="v_t")
+            for j in range(TB):
+                tokens = slice(b * T + j * P, b * T + (j + 1) * P)
+                acc = psum_acc.tile([P, D], F32, name="acc")
+                for c in range(CB):
+                    nc.tensor.matmul(
+                        acc[:], x_bf[c][:, tokens], weights["v"][:, c, :],
+                        start=(c == 0), stop=(c == CB - 1),
+                    )
+                nc.vector.tensor_tensor(v_t[:, j, :], acc[:], bv_rows[:], ADD)
+
+            o = sequence.tile([P, H, T], BF16, name="o")
+            for h in range(H):
+                head = slice(h * P, (h + 1) * P)
+                a_t = work.tile([P, TB, T], BF16, name="a_t")
+                for i in range(TB):
+                    queries = slice(i * P, (i + 1) * P)
+                    s = psum_s.tile([P, T], F32, name="s")
+                    nc.tensor.matmul(s[:], q[:, h, queries], k[:, h, :], start=True, stop=True)
+
+                    top = stat.tile([P, 1], F32, name="top")
+                    nc.vector.reduce_max(top[:], s[:], axis=ALONG_FREE)
+                    shift = stat.tile([P, 1], F32, name="shift")
+                    nc.vector.tensor_scalar_mul(shift[:], top[:], -SCALE)
+                    e = work.tile([P, T], F32, name="e")
+                    total = stat.tile([P, 1], F32, name="total")
+                    nc.scalar.activation(
+                        e[:], s[:], FUNC.Exp, bias=shift[:], scale=SCALE, accum_out=total[:]
+                    )
+                    inverse = stat.tile([P, 1], F32, name="inverse")
+                    nc.vector.reciprocal(inverse[:], total[:])
+                    a = work.tile([P, T], BF16, name="a")
+                    nc.vector.tensor_scalar_mul(a[:], e[:], inverse[:])
+
+                    a_t_ps = psum_t.tile([P, TB, P], BF16, name="a_t_ps")
+                    for j in range(TB):
+                        nc.tensor.transpose(
+                            a_t_ps[:, j, :], a[:, j * P : (j + 1) * P], identity_b[:]
+                        )
+                    nc.scalar.copy(a_t[:, :, queries], a_t_ps[:])
+
+                o_ps = psum_o.tile([P, T], F32, name="o_ps")
+                for j in range(TB):
+                    nc.tensor.matmul(
+                        o_ps[:], v_t[:, j, head], a_t[:, j, :],
+                        start=(j == 0), stop=(j == TB - 1),
+                    )
+                nc.scalar.copy(o[:, h, :], o_ps[:])
+
+            for m in range(CB):
+                acc = psum_acc.tile([P, T], F32, name="acc")
+                for h in range(H):
+                    nc.tensor.matmul(
+                        acc[:], weights["o"][:, h, m * P : (m + 1) * P], o[:, h, :],
+                        start=(h == 0), stop=(h == H - 1),
+                    )
+                result = work.tile([P, T], F32, name="result")
+                nc.vector.scalar_tensor_tensor(
+                    result[:], acc[:], bo_col[m], x[m][:, seq], ADD, ADD
+                )
+                nc.sync.dma_start(out[m * P : (m + 1) * P, seq], result[:])

@@ -19,6 +19,11 @@ TB = T // P
 PER_COLUMN = 16
 SCALE = 1.0 / math.sqrt(P)
 
+HEADS = B * H
+STEPS = HEADS * TB
+
+LEAD_QK, LEAD_V, LAG_OUT = 2, 3, 8
+
 FLOPS = 4 * 2 * D * D * B * T + 2 * B * H * 2 * T * T * P
 
 
@@ -28,7 +33,8 @@ def tile_enhancedtransformertextclassifier_b_kernel(
     nc = tc.nc
     with (
         tc.tile_pool(name="held", bufs=1) as held,
-        tc.tile_pool(name="sequence", bufs=2) as sequence,
+        tc.tile_pool(name="pairs", bufs=4) as pairs,
+        tc.tile_pool(name="sequences", bufs=3) as sequences,
         tc.tile_pool(name="work", bufs=3) as work,
         tc.tile_pool(name="stat", bufs=4) as stat,
         tc.psum_pool(name="psum_acc", bufs=2) as psum_acc,
@@ -39,31 +45,31 @@ def tile_enhancedtransformertextclassifier_b_kernel(
         offsets = held.tile([P, B * T // PER_COLUMN], U16, name="offsets")
         nc.sync.dma_start(offsets[:], offs)
 
+        rows = held.tile([P, P], F32, name="rows")
+        nc.vector.memset(rows[:], 0.0)
+        for r, vector in enumerate((type_emb, bq, bo)):
+            nc.sync.dma_start(
+                rows[r * CB : (r + 1) * CB, :], vector.rearrange("(c p) o -> c (p o)", p=P)
+            )
+
         tok = [held.tile([P, V], F32, name=f"tok{c}") for c in range(CB)]
-        for c in range(CB):
-            nc.sync.dma_start(tok[c][:], tok_emb[c * P : (c + 1) * P, :])
-
         pos = held.tile([P, CB, T], F32, name="pos")
-        for c in range(CB):
-            nc.scalar.dma_start(pos[:, c, :], pos_emb[c * P : (c + 1) * P, :])
-        weights = {}
-        for name, w in (("q", wq), ("k", wk), ("v", wv), ("o", wo)):
-            weights[name] = held.tile([P, CB, D], BF16, name=f"w{name}")
-            nc.scalar.dma_start(weights[name][:], w.rearrange("(c p) m -> p c m", p=P))
-
+        weights = {
+            name: held.tile([P, CB, D], BF16, name=f"w{name}") for name in ("q", "k", "v", "o")
+        }
         bv_rows = held.tile([P, D], F32, name="bv_rows")
-        nc.gpsimd.dma_start(bv_rows[:], bv.rearrange("m o -> (m o)").partition_broadcast(P))
+        for c in range(CB):
+            nc.sync.dma_start(pos[:, c, :], pos_emb[c * P : (c + 1) * P, :])
+            nc.sync.dma_start(tok[c][:], tok_emb[c * P : (c + 1) * P, :])
+        for name, w in (("q", wq), ("k", wk), ("v", wv)):
+            nc.sync.dma_start(weights[name][:], w.rearrange("(c p) m -> p c m", p=P))
+        nc.sync.dma_start(bv_rows[:], bv.rearrange("m o -> (m o)").partition_broadcast(P))
+        nc.sync.dma_start(weights["o"][:], wo.rearrange("(c p) m -> p c m", p=P))
 
         identity_f = held.tile([P, P], F32, name="identity_f")
         make_identity(nc, identity_f[:])
         identity_b = held.tile([P, P], BF16, name="identity_b")
         make_identity(nc, identity_b[:])
-        rows = held.tile([P, P], F32, name="rows")
-        nc.vector.memset(rows[:], 0.0)
-        for n, vector in enumerate((type_emb, bq, bo)):
-            nc.gpsimd.dma_start(
-                rows[n * CB : (n + 1) * CB, :], vector.rearrange("(c p) o -> c (p o)", p=P)
-            )
         acc = psum_acc.tile([P, T], F32, name="acc")
         nc.tensor.transpose(acc[:, 0:P], rows[:], identity_f[:])
         columns = held.tile([P, 3 * CB], F32, name="columns")
@@ -83,88 +89,136 @@ def tile_enhancedtransformertextclassifier_b_kernel(
                 nc.vector.tensor_tensor(
                     x[c][:, seq], tok[c][:].indirect(piece), pos_type[:, c, :], ADD
                 )
-                nc.gpsimd.tensor_copy(x_bf[c][:, seq], x[c][:, seq])
+                nc.scalar.copy(x_bf[c][:, seq], x[c][:, seq])
 
-        for b in range(B):
-            seq = slice(b * T, (b + 1) * T)
+        q, k, v_t, o = {}, {}, {}, {}
 
-            q = sequence.tile([P, H, T], BF16, name="q")
-            k = sequence.tile([P, H, T], BF16, name="k")
-            for h in range(H):
-                head = slice(h * P, (h + 1) * P)
-                acc = psum_acc.tile([P, T], F32, name="acc")
-                for c in range(CB):
-                    nc.tensor.matmul(
-                        acc[:], weights["q"][:, c, head], x_bf[c][:, seq],
-                        start=(c == 0), stop=(c == CB - 1),
-                    )
-                nc.scalar.activation(q[:, h, :], acc[:], FUNC.Identity, bias=bq_col[h])
-                acc = psum_acc.tile([P, T], F32, name="acc")
-                for c in range(CB):
-                    nc.tensor.matmul(
-                        acc[:], weights["k"][:, c, head], x_bf[c][:, seq],
-                        start=(c == 0), stop=(c == CB - 1),
-                    )
-                nc.scalar.copy(k[:, h, :], acc[:])
-
-            v_t = sequence.tile([P, TB, D], BF16, name="v_t")
-            for j in range(TB):
-                tokens = slice(b * T + j * P, b * T + (j + 1) * P)
-                acc = psum_acc.tile([P, D], F32, name="acc")
-                for c in range(CB):
-                    nc.tensor.matmul(
-                        acc[:], x_bf[c][:, tokens], weights["v"][:, c, :],
-                        start=(c == 0), stop=(c == CB - 1),
-                    )
-                nc.vector.tensor_tensor(v_t[:, j, :], acc[:], bv_rows[:], ADD)
-
-            o = sequence.tile([P, H, T], BF16, name="o")
-            for h in range(H):
-                head = slice(h * P, (h + 1) * P)
-                a_t = work.tile([P, TB, T], BF16, name="a_t")
-                for i in range(TB):
-                    queries = slice(i * P, (i + 1) * P)
-                    s = psum_s.tile([P, T], F32, name="s")
-                    nc.tensor.matmul(s[:], q[:, h, queries], k[:, h, :], start=True, stop=True)
-
-                    top = stat.tile([P, 1], F32, name="top")
-                    nc.vector.reduce_max(top[:], s[:], axis=ALONG_FREE)
-                    shift = stat.tile([P, 1], F32, name="shift")
-                    nc.vector.tensor_scalar_mul(shift[:], top[:], -SCALE)
-                    e = work.tile([P, T], F32, name="e")
-                    total = stat.tile([P, 1], F32, name="total")
-                    nc.scalar.activation(
-                        e[:], s[:], FUNC.Exp, bias=shift[:], scale=SCALE, accum_out=total[:]
-                    )
-                    inverse = stat.tile([P, 1], F32, name="inverse")
-                    nc.vector.reciprocal(inverse[:], total[:])
-                    a = work.tile([P, T], BF16, name="a")
-                    nc.vector.tensor_scalar_mul(a[:], e[:], inverse[:])
-
-                    a_t_ps = psum_t.tile([P, TB, P], BF16, name="a_t_ps")
-                    for j in range(TB):
-                        nc.tensor.transpose(
-                            a_t_ps[:, j, :], a[:, j * P : (j + 1) * P], identity_b[:]
-                        )
-                    nc.scalar.copy(a_t[:, :, queries], a_t_ps[:])
-
-                o_ps = psum_o.tile([P, T], F32, name="o_ps")
-                for j in range(TB):
-                    nc.tensor.matmul(
-                        o_ps[:], v_t[:, j, head], a_t[:, j, :],
-                        start=(j == 0), stop=(j == TB - 1),
-                    )
-                nc.scalar.copy(o[:, h, :], o_ps[:])
-
-            for m in range(CB):
-                acc = psum_acc.tile([P, T], F32, name="acc")
-                for h in range(H):
-                    nc.tensor.matmul(
-                        acc[:], weights["o"][:, h, m * P : (m + 1) * P], o[:, h, :],
-                        start=(h == 0), stop=(h == H - 1),
-                    )
-                result = work.tile([P, T], F32, name="result")
-                nc.vector.scalar_tensor_tensor(
-                    result[:], acc[:], bo_col[m], x[m][:, seq], ADD, ADD
+        def project_q(g):
+            b, h = divmod(g, H)
+            acc = psum_acc.tile([P, T], F32, name="acc")
+            for c in range(CB):
+                nc.tensor.matmul(
+                    acc[:], weights["q"][:, c, h * P : (h + 1) * P],
+                    x_bf[c][:, b * T : (b + 1) * T], start=(c == 0), stop=(c == CB - 1),
                 )
-                nc.sync.dma_start(out[m * P : (m + 1) * P, seq], result[:])
+            q[g] = pairs.tile([P, T], BF16, name="q")
+            nc.scalar.activation(q[g][:], acc[:], FUNC.Identity, bias=bq_col[h])
+
+        def project_k(g):
+            b, h = divmod(g, H)
+            acc = psum_acc.tile([P, T], F32, name="acc")
+            for c in range(CB):
+                nc.tensor.matmul(
+                    acc[:], weights["k"][:, c, h * P : (h + 1) * P],
+                    x_bf[c][:, b * T : (b + 1) * T], start=(c == 0), stop=(c == CB - 1),
+                )
+            k[g] = pairs.tile([P, T], BF16, name="k")
+            nc.scalar.copy(k[g][:], acc[:])
+
+        def project_v(r):
+            b, j = divmod(r, TB)
+            if j == 0:
+                v_t[b] = sequences.tile([P, TB, D], BF16, name="v_t")
+            acc = psum_acc.tile([P, D], F32, name="acc")
+            for c in range(CB):
+                nc.tensor.matmul(
+                    acc[:], x_bf[c][:, r * P : (r + 1) * P], weights["v"][:, c, :],
+                    start=(c == 0), stop=(c == CB - 1),
+                )
+            nc.vector.tensor_tensor(v_t[b][:, j, :], acc[:], bv_rows[:], ADD)
+
+        def output(r):
+            b, m = divmod(r, CB)
+            acc = psum_acc.tile([P, T], F32, name="acc")
+            for h in range(H):
+                nc.tensor.matmul(
+                    acc[:], weights["o"][:, h, m * P : (m + 1) * P], o[b][:, h, :],
+                    start=(h == 0), stop=(h == H - 1),
+                )
+            result = work.tile([P, T], F32, name="result")
+            nc.vector.scalar_tensor_tensor(
+                result[:], acc[:], bo_col[m], x[m][:, b * T : (b + 1) * T], ADD, ADD
+            )
+            nc.sync.dma_start(out[m * P : (m + 1) * P, b * T : (b + 1) * T], result[:])
+
+        def projection(n):
+            g, i = divmod(n, TB)
+            if i == 0 and 0 <= g + LEAD_QK < HEADS:
+                project_q(g + LEAD_QK)
+            if i == 1 and 0 <= g + LEAD_QK < HEADS:
+                project_k(g + LEAD_QK)
+            if i == 2 and 0 <= g + LEAD_V < HEADS:
+                project_v(g + LEAD_V)
+            if i == 3 and 0 <= g - LAG_OUT < HEADS:
+                output(g - LAG_OUT)
+
+        s, shift, e, total, a, a_t_ps, a_t = {}, {}, {}, {}, {}, {}, {}
+
+        def scores(n):
+            g, i = divmod(n, TB)
+            s[n] = psum_s.tile([P, T], F32, name="s")
+            nc.tensor.matmul(s[n][:], q[g][:, i * P : (i + 1) * P], k[g][:], start=True, stop=True)
+
+        def find_shift(n):
+            top = stat.tile([P, 1], F32, name="top")
+            nc.vector.reduce_max(top[:], s[n][:], axis=ALONG_FREE)
+            shift[n] = stat.tile([P, 1], F32, name="shift")
+            nc.vector.tensor_scalar_mul(shift[n][:], top[:], -SCALE)
+
+        def exponentials(n):
+            e[n] = work.tile([P, T], F32, name="e")
+            total[n] = stat.tile([P, 1], F32, name="total")
+            nc.scalar.activation(
+                e[n][:], s[n][:], FUNC.Exp, bias=shift[n][:], scale=SCALE, accum_out=total[n][:]
+            )
+
+        def normalise(n):
+            inverse = stat.tile([P, 1], F32, name="inverse")
+            nc.vector.reciprocal(inverse[:], total[n][:])
+            a[n] = work.tile([P, T], BF16, name="a")
+            nc.vector.tensor_scalar_mul(a[n][:], e[n][:], inverse[:])
+
+        def flip(n):
+            a_t_ps[n] = psum_t.tile([P, TB, P], BF16, name="a_t_ps")
+            for j in range(TB):
+                nc.tensor.transpose(
+                    a_t_ps[n][:, j, :], a[n][:, j * P : (j + 1) * P], identity_b[:]
+                )
+
+        def keep(n):
+            g, i = divmod(n, TB)
+            if i == 0:
+                a_t[g] = work.tile([P, TB, T], BF16, name="a_t")
+            nc.scalar.copy(a_t[g][:, :, i * P : (i + 1) * P], a_t_ps[n][:])
+
+        def weigh(g):
+            b, h = divmod(g, H)
+            if h == 0:
+                o[b] = sequences.tile([P, H, T], BF16, name="o")
+            o_ps = psum_o.tile([P, T], F32, name="o_ps")
+            for j in range(TB):
+                nc.tensor.matmul(
+                    o_ps[:], v_t[b][:, j, h * P : (h + 1) * P], a_t[g][:, j, :],
+                    start=(j == 0), stop=(j == TB - 1),
+                )
+            nc.scalar.copy(o[b][:, h, :], o_ps[:])
+
+        def due(n):
+            return 0 <= n < STEPS
+
+        for n in range(-LEAD_V * TB, (HEADS + LAG_OUT) * TB):
+            if due(n + 3):
+                scores(n + 3)
+            if due(n + 2):
+                find_shift(n + 2)
+            if due(n + 1):
+                exponentials(n + 1)
+            if due(n):
+                normalise(n)
+            projection(n)
+            if due(n - 1):
+                flip(n - 1)
+            if due(n - 2):
+                keep(n - 2)
+            if due(n - 3) and (n - 3) % TB == TB - 1:
+                weigh((n - 3) // TB)

@@ -5,6 +5,7 @@ from concourse.masks import make_identity
 
 F32, BF16, U16 = mybir.dt.float32, mybir.dt.bfloat16, mybir.dt.uint16
 ADD = mybir.AluOpType.add
+MULT = mybir.AluOpType.mult
 FUNC = mybir.ActivationFunctionType
 ALONG_FREE = mybir.AxisListType.X
 
@@ -176,7 +177,7 @@ def tile_enhancedtransformertextclassifier_b_kernel(
             inverse = stat.tile([P, 1], F32, name="inverse")
             nc.vector.reciprocal(inverse[:], total[n][:])
             a[n] = work.tile([P, T], BF16, name="a")
-            nc.vector.tensor_scalar_mul(a[n][:], e[n][:], inverse[:])
+            nc.gpsimd.tensor_scalar(a[n][:], e[n][:], inverse[:], 0.0, MULT, ADD)
 
         def flip(n):
             a_t_ps[n] = psum_t.tile([P, TB, P], BF16, name="a_t_ps")
@@ -189,7 +190,7 @@ def tile_enhancedtransformertextclassifier_b_kernel(
             g, i = divmod(n, TB)
             if i == 0:
                 a_t[g] = work.tile([P, TB, T], BF16, name="a_t")
-            nc.scalar.copy(a_t[g][:, :, i * P : (i + 1) * P], a_t_ps[n][:])
+            nc.vector.tensor_copy(a_t[g][:, :, i * P : (i + 1) * P], a_t_ps[n][:])
 
         def weigh(g):
             b, h = divmod(g, H)

@@ -25,6 +25,8 @@ STEPS = HEADS * TB
 
 LEAD_QK, LEAD_V, LAG_OUT = 2, 3, 8
 
+EARLY = 8
+
 FLOPS = 4 * 2 * D * D * B * T + 2 * B * H * 2 * T * T * P
 
 
@@ -62,10 +64,10 @@ def tile_enhancedtransformertextclassifier_b_kernel(
         for c in range(CB):
             nc.sync.dma_start(pos[:, c, :], pos_emb[c * P : (c + 1) * P, :])
             nc.sync.dma_start(tok[c][:], tok_emb[c * P : (c + 1) * P, :])
-        for name, w in (("q", wq), ("k", wk), ("v", wv)):
-            nc.sync.dma_start(weights[name][:], w.rearrange("(c p) m -> p c m", p=P))
+            nc.sync.dma_start(weights["v"][:, c, :], wv[c * P : (c + 1) * P, :])
         nc.sync.dma_start(bv_rows[:], bv.rearrange("m o -> (m o)").partition_broadcast(P))
-        nc.sync.dma_start(weights["o"][:], wo.rearrange("(c p) m -> p c m", p=P))
+        for name, w in (("q", wq), ("k", wk), ("o", wo)):
+            nc.sync.dma_start(weights[name][:], w.rearrange("(c p) m -> p c m", p=P))
 
         identity_f = held.tile([P, P], F32, name="identity_f")
         make_identity(nc, identity_f[:])
@@ -82,51 +84,62 @@ def tile_enhancedtransformertextclassifier_b_kernel(
         pos_type = held.tile([P, CB, T], F32, name="pos_type")
         x = [held.tile([P, B * T], F32, name=f"x{c}") for c in range(CB)]
         x_bf = [held.tile([P, B * T], BF16, name=f"x_bf{c}") for c in range(CB)]
-        for c in range(CB):
-            nc.vector.tensor_scalar_add(pos_type[:, c, :], pos[:, c, :], type_col[c])
-            for b in range(B):
-                seq = slice(b * T, (b + 1) * T)
-                piece = offsets[:, b * T // PER_COLUMN : (b + 1) * T // PER_COLUMN]
-                nc.vector.tensor_tensor(
-                    x[c][:, seq], tok[c][:].indirect(piece), pos_type[:, c, :], ADD
-                )
-                nc.scalar.copy(x_bf[c][:, seq], x[c][:, seq])
+
+        def look_up(c, b):
+            seq = slice(b * T, (b + 1) * T)
+            piece = offsets[:, b * T // PER_COLUMN : (b + 1) * T // PER_COLUMN]
+            nc.vector.tensor_tensor(
+                x[c][:, seq], tok[c][:].indirect(piece), pos_type[:, c, :], ADD
+            )
+            nc.scalar.copy(x_bf[c][:, seq], x[c][:, seq])
 
         q, k, v_t, o = {}, {}, {}, {}
 
-        def project_q(g):
-            b, h = divmod(g, H)
+        def add_block(kind, index, acc, c):
+            if kind == "v":
+                stationary = x_bf[c][:, index * P : (index + 1) * P]
+                moving = weights["v"][:, c, :]
+            else:
+                b, h = divmod(index, H)
+                stationary = weights[kind][:, c, h * P : (h + 1) * P]
+                moving = x_bf[c][:, b * T : (b + 1) * T]
+            nc.tensor.matmul(acc[:], stationary, moving, start=(c == 0), stop=(c == CB - 1))
+
+        def round_off(kind, index, acc):
+            if kind == "q":
+                q[index] = pairs.tile([P, T], BF16, name="q")
+                nc.scalar.activation(q[index][:], acc[:], FUNC.Identity, bias=bq_col[index % H])
+            if kind == "k":
+                k[index] = pairs.tile([P, T], BF16, name="k")
+                nc.scalar.copy(k[index][:], acc[:])
+            if kind == "v":
+                b, j = divmod(index, TB)
+                if j == 0:
+                    v_t[b] = sequences.tile([P, TB, D], BF16, name="v_t")
+                nc.vector.tensor_tensor(v_t[b][:, j, :], acc[:], bv_rows[:], ADD)
+
+        def project(kind, index):
+            if not 0 <= index < HEADS or (kind == "v" and index < EARLY):
+                return
             acc = psum_acc.tile([P, T], F32, name="acc")
             for c in range(CB):
-                nc.tensor.matmul(
-                    acc[:], weights["q"][:, c, h * P : (h + 1) * P],
-                    x_bf[c][:, b * T : (b + 1) * T], start=(c == 0), stop=(c == CB - 1),
-                )
-            q[g] = pairs.tile([P, T], BF16, name="q")
-            nc.scalar.activation(q[g][:], acc[:], FUNC.Identity, bias=bq_col[h])
+                add_block(kind, index, acc, c)
+            round_off(kind, index, acc)
 
-        def project_k(g):
-            b, h = divmod(g, H)
-            acc = psum_acc.tile([P, T], F32, name="acc")
-            for c in range(CB):
-                nc.tensor.matmul(
-                    acc[:], weights["k"][:, c, h * P : (h + 1) * P],
-                    x_bf[c][:, b * T : (b + 1) * T], start=(c == 0), stop=(c == CB - 1),
-                )
-            k[g] = pairs.tile([P, T], BF16, name="k")
-            nc.scalar.copy(k[g][:], acc[:])
-
-        def project_v(r):
-            b, j = divmod(r, TB)
-            if j == 0:
-                v_t[b] = sequences.tile([P, TB, D], BF16, name="v_t")
-            acc = psum_acc.tile([P, D], F32, name="acc")
-            for c in range(CB):
-                nc.tensor.matmul(
-                    acc[:], x_bf[c][:, r * P : (r + 1) * P], weights["v"][:, c, :],
-                    start=(c == 0), stop=(c == CB - 1),
-                )
-            nc.vector.tensor_tensor(v_t[b][:, j, :], acc[:], bv_rows[:], ADD)
+        early_acc = (
+            [psum_acc.tile([P, T], F32, name="acc") for i in range(2)]
+            + [psum_s.tile([P, T], F32, name="s") for i in range(3)]
+            + [psum_t.tile([P, T], F32, name="a_t_ps") for i in range(2)]
+            + [psum_o.tile([P, T], F32, name="o_ps")]
+        )
+        for c in range(CB):
+            nc.vector.tensor_scalar_add(pos_type[:, c, :], pos[:, c, :], type_col[c])
+            for b in range(B if c < CB - 1 else EARLY // TB):
+                look_up(c, b)
+                for r in range(b * TB, min((b + 1) * TB, EARLY)):
+                    add_block("v", r, early_acc[r], c)
+        for r in range(EARLY):
+            round_off("v", r, early_acc[r])
 
         def output(r):
             b, m = divmod(r, CB)
@@ -144,12 +157,12 @@ def tile_enhancedtransformertextclassifier_b_kernel(
 
         def projection(n):
             g, i = divmod(n, TB)
-            if i == 0 and 0 <= g + LEAD_QK < HEADS:
-                project_q(g + LEAD_QK)
-            if i == 1 and 0 <= g + LEAD_QK < HEADS:
-                project_k(g + LEAD_QK)
-            if i == 2 and 0 <= g + LEAD_V < HEADS:
-                project_v(g + LEAD_V)
+            if i == 0:
+                project("q", g + LEAD_QK)
+            if i == 1:
+                project("k", g + LEAD_QK)
+            if i == 2:
+                project("v", g + LEAD_V)
             if i == 3 and 0 <= g - LAG_OUT < HEADS:
                 output(g - LAG_OUT)
 
@@ -223,3 +236,5 @@ def tile_enhancedtransformertextclassifier_b_kernel(
                 keep(n - 2)
             if due(n - 3) and (n - 3) % TB == TB - 1:
                 weigh((n - 3) // TB)
+            if due(n) and n % (H * TB) == 0 and EARLY // TB <= n // (H * TB) + 1 < B:
+                look_up(CB - 1, n // (H * TB) + 1)

@@ -18,6 +18,7 @@ H = 4
 CB = D // P
 TB = T // P
 PER_COLUMN = 16
+PAIR = 2
 SCALE = 1.0 / math.sqrt(P)
 
 HEADS = B * H
@@ -71,8 +72,6 @@ def tile_enhancedtransformertextclassifier_b_kernel(
 
         identity_f = held.tile([P, P], F32, name="identity_f")
         make_identity(nc, identity_f[:])
-        identity_b = held.tile([P, P], BF16, name="identity_b")
-        make_identity(nc, identity_b[:])
         acc = psum_acc.tile([P, T], F32, name="acc")
         nc.tensor.transpose(acc[:, 0:P], rows[:], identity_f[:])
         columns = held.tile([P, 3 * CB], F32, name="columns")
@@ -95,9 +94,13 @@ def tile_enhancedtransformertextclassifier_b_kernel(
 
         q, k, v_t, o = {}, {}, {}, {}
 
+        def tokens_of(r):
+            half, parity = divmod(r, PAIR)
+            return slice(half * PAIR * P + parity, (half + 1) * PAIR * P, PAIR)
+
         def add_block(kind, index, acc, c):
             if kind == "v":
-                stationary = x_bf[c][:, index * P : (index + 1) * P]
+                stationary = x_bf[c][:, tokens_of(index)]
                 moving = weights["v"][:, c, :]
             else:
                 b, h = divmod(index, H)
@@ -193,16 +196,15 @@ def tile_enhancedtransformertextclassifier_b_kernel(
             nc.gpsimd.tensor_scalar(a[n][:], e[n][:], inverse[:], 0.0, MULT, ADD)
 
         def flip(n):
-            a_t_ps[n] = psum_t.tile([P, TB, P], BF16, name="a_t_ps")
-            for j in range(TB):
-                nc.tensor.transpose(
-                    a_t_ps[n][:, j, :], a[n][:, j * P : (j + 1) * P], identity_b[:]
-                )
+            a_t_ps[n] = psum_t.tile([P, TB // PAIR, P], F32, name="a_t_ps")
+            for half in range(TB // PAIR):
+                words = a[n][:, half * PAIR * P : (half + 1) * PAIR * P].bitcast(F32)
+                nc.tensor.transpose(a_t_ps[n][:, half, :], words, identity_f[:])
 
         def keep(n):
             g, i = divmod(n, TB)
             if i == 0:
-                a_t[g] = work.tile([P, TB, T], BF16, name="a_t")
+                a_t[g] = work.tile([P, TB // PAIR, T], F32, name="a_t")
             nc.vector.tensor_copy(a_t[g][:, :, i * P : (i + 1) * P], a_t_ps[n][:])
 
         def weigh(g):
@@ -211,8 +213,10 @@ def tile_enhancedtransformertextclassifier_b_kernel(
                 o[b] = sequences.tile([P, H, T], BF16, name="o")
             o_ps = psum_o.tile([P, T], F32, name="o_ps")
             for j in range(TB):
+                half, parity = divmod(j, PAIR)
                 nc.tensor.matmul(
-                    o_ps[:], v_t[b][:, j, h * P : (h + 1) * P], a_t[g][:, j, :],
+                    o_ps[:], v_t[b][:, j, h * P : (h + 1) * P],
+                    a_t[g][:, half, :].bitcast(BF16)[:, parity::PAIR],
                     start=(j == 0), stop=(j == TB - 1),
                 )
             nc.scalar.copy(o[b][:, h, :], o_ps[:])

@@ -24,9 +24,10 @@ SCALE = 1.0 / math.sqrt(P)
 HEADS = B * H
 STEPS = HEADS * TB
 
-LEAD_QK, LEAD_V, LAG_OUT = 2, 3, 8
+LEAD_QK, LEAD_V, LAG_OUT = 2, 3, 5
 
 EARLY = 8
+HALF = 2
 
 FLOPS = 4 * 2 * D * D * B * T + 2 * B * H * 2 * T * T * P
 
@@ -98,7 +99,7 @@ def tile_enhancedtransformertextclassifier_b_kernel(
             half, parity = divmod(r, PAIR)
             return slice(half * PAIR * P + parity, (half + 1) * PAIR * P, PAIR)
 
-        def add_block(kind, index, acc, c):
+        def add_block(kind, index, acc, c, first=0, last=CB - 1):
             if kind == "v":
                 stationary = x_bf[c][:, tokens_of(index)]
                 moving = weights["v"][:, c, :]
@@ -106,7 +107,7 @@ def tile_enhancedtransformertextclassifier_b_kernel(
                 b, h = divmod(index, H)
                 stationary = weights[kind][:, c, h * P : (h + 1) * P]
                 moving = x_bf[c][:, b * T : (b + 1) * T]
-            nc.tensor.matmul(acc[:], stationary, moving, start=(c == 0), stop=(c == CB - 1))
+            nc.tensor.matmul(acc[:], stationary, moving, start=(c == first), stop=(c == last))
 
         def round_off(kind, index, acc):
             if kind == "q":
@@ -119,27 +120,56 @@ def tile_enhancedtransformertextclassifier_b_kernel(
                 b, j = divmod(index, TB)
                 if j == 0:
                     v_t[b] = sequences.tile([P, TB, D], BF16, name="v_t")
+                if index in parked:
+                    whole = work.tile([P, D], F32, name="whole")
+                    nc.vector.tensor_tensor(whole[:], acc[:], parked[index][:], ADD)
+                    acc = whole
                 nc.vector.tensor_tensor(v_t[b][:, j, :], acc[:], bv_rows[:], ADD)
 
         def project(kind, index):
             if not 0 <= index < HEADS or (kind == "v" and index < EARLY):
                 return
+            first = HALF if kind == "v" else 0
             acc = psum_acc.tile([P, T], F32, name="acc")
-            for c in range(CB):
-                add_block(kind, index, acc, c)
+            for c in range(first, CB):
+                add_block(kind, index, acc, c, first)
             round_off(kind, index, acc)
 
-        early_acc = (
-            [psum_acc.tile([P, T], F32, name="acc") for i in range(2)]
-            + [psum_s.tile([P, T], F32, name="s") for i in range(3)]
-            + [psum_t.tile([P, T], F32, name="a_t_ps") for i in range(2)]
-            + [psum_o.tile([P, T], F32, name="o_ps")]
-        )
-        for c in range(CB):
+        def all_banks():
+            return (
+                [psum_acc.tile([P, T], F32, name="acc") for i in range(2)]
+                + [psum_s.tile([P, T], F32, name="s") for i in range(3)]
+                + [psum_t.tile([P, T], F32, name="a_t_ps") for i in range(2)]
+                + [psum_o.tile([P, T], F32, name="o_ps")]
+            )
+
+        def blocks_of(b):
+            return range(b * TB, (b + 1) * TB)
+
+        parked = {}
+        late_acc = all_banks()
+        for c in range(HALF):
             nc.vector.tensor_scalar_add(pos_type[:, c, :], pos[:, c, :], type_col[c])
-            for b in range(B if c < CB - 1 else EARLY // TB):
+            for b in (2, 3):
                 look_up(c, b)
-                for r in range(b * TB, min((b + 1) * TB, EARLY)):
+                for r in blocks_of(b):
+                    add_block("v", r, late_acc[r - EARLY], c, 0, HALF - 1)
+            for b in (0, 1):
+                look_up(c, b)
+        for r in range(EARLY, 2 * EARLY):
+            parked[r] = held.tile([P, D], F32, name=f"parked{r}")
+            if r % 2 == 0:
+                nc.scalar.copy(parked[r][:], late_acc[r - EARLY][:])
+            else:
+                nc.vector.tensor_copy(parked[r][:], late_acc[r - EARLY][:])
+        early_acc = all_banks()
+        for c in range(CB):
+            if c >= HALF:
+                nc.vector.tensor_scalar_add(pos_type[:, c, :], pos[:, c, :], type_col[c])
+            for b in (0, 1):
+                if c >= HALF:
+                    look_up(c, b)
+                for r in blocks_of(b):
                     add_block("v", r, early_acc[r], c)
         for r in range(EARLY):
             round_off("v", r, early_acc[r])
@@ -240,5 +270,6 @@ def tile_enhancedtransformertextclassifier_b_kernel(
                 keep(n - 2)
             if due(n - 3) and (n - 3) % TB == TB - 1:
                 weigh((n - 3) // TB)
-            if due(n) and n % (H * TB) == 0 and EARLY // TB <= n // (H * TB) + 1 < B:
-                look_up(CB - 1, n // (H * TB) + 1)
+            b, turn = divmod(n, H * TB)
+            if 1 <= b < B - 1 and turn % TB == 0 and HALF + turn // TB < CB:
+                look_up(HALF + turn // TB, b + 1)

@@ -67,8 +67,9 @@ def tile_enhancedtransformertextclassifier_b_kernel(
             nc.sync.dma_start(pos[:, c, :], pos_emb[c * P : (c + 1) * P, :])
             nc.sync.dma_start(tok[c][:], tok_emb[c * P : (c + 1) * P, :])
             nc.sync.dma_start(weights["v"][:, c, :], wv[c * P : (c + 1) * P, :])
+        nc.sync.dma_start(weights["q"][:], wq.rearrange("(c p) m -> p c m", p=P))
         nc.sync.dma_start(bv_rows[:], bv.rearrange("m o -> (m o)").partition_broadcast(P))
-        for name, w in (("q", wq), ("k", wk), ("o", wo)):
+        for name, w in (("k", wk), ("o", wo)):
             nc.sync.dma_start(weights[name][:], w.rearrange("(c p) m -> p c m", p=P))
 
         identity_f = held.tile([P, P], F32, name="identity_f")
@@ -120,11 +121,8 @@ def tile_enhancedtransformertextclassifier_b_kernel(
                 b, j = divmod(index, TB)
                 if j == 0:
                     v_t[b] = sequences.tile([P, TB, D], BF16, name="v_t")
-                if index in parked:
-                    whole = work.tile([P, D], F32, name="whole")
-                    nc.vector.tensor_tensor(whole[:], acc[:], parked[index][:], ADD)
-                    acc = whole
-                nc.vector.tensor_tensor(v_t[b][:, j, :], acc[:], bv_rows[:], ADD)
+                rest = parked[index] if index in parked else bv_rows
+                nc.vector.tensor_tensor(v_t[b][:, j, :], acc[:], rest[:], ADD)
 
         def project(kind, index):
             if not 0 <= index < HEADS or (kind == "v" and index < EARLY):
@@ -162,6 +160,7 @@ def tile_enhancedtransformertextclassifier_b_kernel(
                 nc.scalar.copy(parked[r][:], late_acc[r - EARLY][:])
             else:
                 nc.vector.tensor_copy(parked[r][:], late_acc[r - EARLY][:])
+            nc.gpsimd.tensor_tensor(parked[r][:], parked[r][:], bv_rows[:], ADD)
         early_acc = all_banks()
         for c in range(CB):
             if c >= HALF:

@@ -40,8 +40,8 @@ def tile_enhancedtransformertextclassifier_b_kernel(
         tc.tile_pool(name="held", bufs=1) as held,
         tc.tile_pool(name="pairs", bufs=4) as pairs,
         tc.tile_pool(name="sequences", bufs=3) as sequences,
-        tc.tile_pool(name="work", bufs=3) as work,
-        tc.tile_pool(name="stat", bufs=4) as stat,
+        tc.tile_pool(name="work", bufs=4) as work,
+        tc.tile_pool(name="stat", bufs=6) as stat,
         tc.psum_pool(name="psum_acc", bufs=2) as psum_acc,
         tc.psum_pool(name="psum_s", bufs=3) as psum_s,
         tc.psum_pool(name="psum_t", bufs=2) as psum_t,

@@ -52,7 +52,7 @@ def tile_enhancedtransformertextclassifier_b_kernel(
 
         rows = held.tile([P, P], F32, name="rows")
         nc.vector.memset(rows[:], 0.0)
-        for r, vector in enumerate((type_emb, bq, bo)):
+        for r, vector in enumerate((type_emb, bq, bo, bv)):
             nc.sync.dma_start(
                 rows[r * CB : (r + 1) * CB, :], vector.rearrange("(c p) o -> c (p o)", p=P)
             )
@@ -62,25 +62,23 @@ def tile_enhancedtransformertextclassifier_b_kernel(
         weights = {
             name: held.tile([P, CB, D], BF16, name=f"w{name}") for name in ("q", "k", "v", "o")
         }
-        bv_rows = held.tile([P, D], F32, name="bv_rows")
         for c in range(CB):
             nc.sync.dma_start(pos[:, c, :], pos_emb[c * P : (c + 1) * P, :])
             nc.sync.dma_start(tok[c][:], tok_emb[c * P : (c + 1) * P, :])
             nc.sync.dma_start(weights["v"][:, c, :], wv[c * P : (c + 1) * P, :])
-        nc.sync.dma_start(weights["q"][:], wq.rearrange("(c p) m -> p c m", p=P))
-        nc.sync.dma_start(bv_rows[:], bv.rearrange("m o -> (m o)").partition_broadcast(P))
-        for name, w in (("k", wk), ("o", wo)):
+        for name, w in (("q", wq), ("k", wk), ("o", wo)):
             nc.sync.dma_start(weights[name][:], w.rearrange("(c p) m -> p c m", p=P))
 
         identity_f = held.tile([P, P], F32, name="identity_f")
         make_identity(nc, identity_f[:])
         acc = psum_acc.tile([P, T], F32, name="acc")
         nc.tensor.transpose(acc[:, 0:P], rows[:], identity_f[:])
-        columns = held.tile([P, 3 * CB], F32, name="columns")
-        nc.vector.tensor_copy(columns[:], acc[:, 0 : 3 * CB])
+        columns = held.tile([P, 4 * CB], F32, name="columns")
+        nc.vector.tensor_copy(columns[:], acc[:, 0 : 4 * CB])
         type_col = [columns[:, c : c + 1] for c in range(CB)]
         bq_col = [columns[:, CB + c : CB + c + 1] for c in range(CB)]
         bo_col = [columns[:, 2 * CB + c : 2 * CB + c + 1] for c in range(CB)]
+        bv_col = [columns[:, 3 * CB + c : 3 * CB + c + 1] for c in range(CB)]
 
         pos_type = held.tile([P, CB, T], F32, name="pos_type")
         x = [held.tile([P, B * T], F32, name=f"x{c}") for c in range(CB)]
@@ -121,8 +119,10 @@ def tile_enhancedtransformertextclassifier_b_kernel(
                 b, j = divmod(index, TB)
                 if j == 0:
                     v_t[b] = sequences.tile([P, TB, D], BF16, name="v_t")
-                rest = parked[index] if index in parked else bv_rows
-                nc.vector.tensor_tensor(v_t[b][:, j, :], acc[:], rest[:], ADD)
+                if index in parked:
+                    nc.vector.tensor_tensor(v_t[b][:, j, :], acc[:], parked[index][:], ADD)
+                else:
+                    nc.vector.tensor_copy(v_t[b][:, j, :], acc[:])
 
         def project(kind, index):
             if not 0 <= index < HEADS or (kind == "v" and index < EARLY):
@@ -160,7 +160,6 @@ def tile_enhancedtransformertextclassifier_b_kernel(
                 nc.scalar.copy(parked[r][:], late_acc[r - EARLY][:])
             else:
                 nc.vector.tensor_copy(parked[r][:], late_acc[r - EARLY][:])
-            nc.gpsimd.tensor_tensor(parked[r][:], parked[r][:], bv_rows[:], ADD)
         early_acc = all_banks()
         for c in range(CB):
             if c >= HALF:
@@ -248,7 +247,7 @@ def tile_enhancedtransformertextclassifier_b_kernel(
                     a_t[g][:, half, :].bitcast(BF16)[:, parity::PAIR],
                     start=(j == 0), stop=(j == TB - 1),
                 )
-            nc.scalar.copy(o[b][:, h, :], o_ps[:])
+            nc.scalar.activation(o[b][:, h, :], o_ps[:], FUNC.Identity, bias=bv_col[h])
 
         def due(n):
             return 0 <= n < STEPS

@@ -27,7 +27,8 @@ STEPS = HEADS * TB
 LEAD_QK, LEAD_V, LAG_OUT = 2, 3, 5
 
 EARLY = 8
-HALF = 2
+PARKED_CB = (0, 1, 2, 3)
+LAST = CB - 1
 
 FLOPS = 4 * 2 * D * D * B * T + 2 * B * H * 2 * T * T * P
 
@@ -50,21 +51,21 @@ def tile_enhancedtransformertextclassifier_b_kernel(
         offsets = held.tile([P, B * T // PER_COLUMN], U16, name="offsets")
         nc.sync.dma_start(offsets[:], offs)
 
-        rows = held.tile([P, P], F32, name="rows")
-        nc.vector.memset(rows[:], 0.0)
-        for r, vector in enumerate((type_emb, bq, bo, bv)):
-            nc.sync.dma_start(
-                rows[r * CB : (r + 1) * CB, :], vector.rearrange("(c p) o -> c (p o)", p=P)
-            )
-
         tok = [held.tile([P, V], F32, name=f"tok{c}") for c in range(CB)]
         pos = held.tile([P, CB, T], F32, name="pos")
         weights = {
             name: held.tile([P, CB, D], BF16, name=f"w{name}") for name in ("q", "k", "v", "o")
         }
+        rows = held.tile([P, P], F32, name="rows")
+        nc.vector.memset(rows[:], 0.0)
         for c in range(CB):
             nc.sync.dma_start(pos[:, c, :], pos_emb[c * P : (c + 1) * P, :])
             nc.sync.dma_start(tok[c][:], tok_emb[c * P : (c + 1) * P, :])
+            if c == 0:
+                for r, vector in enumerate((type_emb, bq, bv, bo)):
+                    nc.sync.dma_start(
+                        rows[r * CB : (r + 1) * CB, :], vector.rearrange("(c p) o -> c (p o)", p=P)
+                    )
             nc.sync.dma_start(weights["v"][:, c, :], wv[c * P : (c + 1) * P, :])
         for name, w in (("q", wq), ("k", wk), ("o", wo)):
             nc.sync.dma_start(weights[name][:], w.rearrange("(c p) m -> p c m", p=P))
@@ -74,23 +75,24 @@ def tile_enhancedtransformertextclassifier_b_kernel(
         acc = psum_acc.tile([P, T], F32, name="acc")
         nc.tensor.transpose(acc[:, 0:P], rows[:], identity_f[:])
         columns = held.tile([P, 4 * CB], F32, name="columns")
-        nc.vector.tensor_copy(columns[:], acc[:, 0 : 4 * CB])
+        nc.scalar.copy(columns[:], acc[:, 0 : 4 * CB])
         type_col = [columns[:, c : c + 1] for c in range(CB)]
         bq_col = [columns[:, CB + c : CB + c + 1] for c in range(CB)]
-        bo_col = [columns[:, 2 * CB + c : 2 * CB + c + 1] for c in range(CB)]
-        bv_col = [columns[:, 3 * CB + c : 3 * CB + c + 1] for c in range(CB)]
+        bv_col = [columns[:, 2 * CB + c : 2 * CB + c + 1] for c in range(CB)]
+        type_bo = held.tile([P, CB], F32, name="type_bo")
+        nc.vector.tensor_tensor(type_bo[:], columns[:, 3 * CB :], columns[:, 0:CB], ADD)
+        type_bo_col = [type_bo[:, c : c + 1] for c in range(CB)]
 
-        pos_type = held.tile([P, CB, T], F32, name="pos_type")
         x = [held.tile([P, B * T], F32, name=f"x{c}") for c in range(CB)]
         x_bf = [held.tile([P, B * T], BF16, name=f"x_bf{c}") for c in range(CB)]
 
-        def look_up(c, b):
-            seq = slice(b * T, (b + 1) * T)
-            piece = offsets[:, b * T // PER_COLUMN : (b + 1) * T // PER_COLUMN]
-            nc.vector.tensor_tensor(
-                x[c][:, seq], tok[c][:].indirect(piece), pos_type[:, c, :], ADD
-            )
-            nc.scalar.copy(x_bf[c][:, seq], x[c][:, seq])
+        def look_up(c, b, part=0, parts=1):
+            first, count = b * T + part * T // parts, T // parts
+            seq = slice(first, first + count)
+            piece = offsets[:, first // PER_COLUMN : (first + count) // PER_COLUMN]
+            here = pos[:, c, part * count : (part + 1) * count]
+            nc.vector.tensor_tensor(x[c][:, seq], tok[c][:].indirect(piece), here, ADD)
+            nc.scalar.activation(x_bf[c][:, seq], x[c][:, seq], FUNC.Identity, bias=type_col[c])
 
         q, k, v_t, o = {}, {}, {}, {}
 
@@ -122,69 +124,101 @@ def tile_enhancedtransformertextclassifier_b_kernel(
                 if index in parked:
                     nc.vector.tensor_tensor(v_t[b][:, j, :], acc[:], parked[index][:], ADD)
                 else:
-                    nc.vector.tensor_copy(v_t[b][:, j, :], acc[:])
+                    nc.scalar.copy(v_t[b][:, j, :], acc[:])
 
         def project(kind, index):
             if not 0 <= index < HEADS or (kind == "v" and index < EARLY):
                 return
-            first = HALF if kind == "v" else 0
+            first = PARKED_CB[index // TB] if kind == "v" else 0
             acc = psum_acc.tile([P, T], F32, name="acc")
             for c in range(first, CB):
                 add_block(kind, index, acc, c, first)
             round_off(kind, index, acc)
 
-        def all_banks():
-            return (
-                [psum_acc.tile([P, T], F32, name="acc") for i in range(2)]
-                + [psum_s.tile([P, T], F32, name="s") for i in range(3)]
-                + [psum_t.tile([P, T], F32, name="a_t_ps") for i in range(2)]
-                + [psum_o.tile([P, T], F32, name="o_ps")]
-            )
+        sums, parked = {}, {}
 
         def blocks_of(b):
             return range(b * TB, (b + 1) * TB)
 
-        parked = {}
-        late_acc = all_banks()
-        for c in range(HALF):
-            nc.vector.tensor_scalar_add(pos_type[:, c, :], pos[:, c, :], type_col[c])
-            for b in (2, 3):
-                look_up(c, b)
-                for r in blocks_of(b):
-                    add_block("v", r, late_acc[r - EARLY], c, 0, HALF - 1)
-            for b in (0, 1):
-                look_up(c, b)
-        for r in range(EARLY, 2 * EARLY):
-            parked[r] = held.tile([P, D], F32, name=f"parked{r}")
-            if r % 2 == 0:
-                nc.scalar.copy(parked[r][:], late_acc[r - EARLY][:])
+        def open_sums(b):
+            if b % 2 == 0:
+                banks = [psum_acc.tile([P, T], F32, name="acc") for i in range(2)]
+                banks += [psum_s.tile([P, T], F32, name="s") for i in range(2)]
             else:
-                nc.vector.tensor_copy(parked[r][:], late_acc[r - EARLY][:])
-        early_acc = all_banks()
-        for c in range(CB):
-            if c >= HALF:
-                nc.vector.tensor_scalar_add(pos_type[:, c, :], pos[:, c, :], type_col[c])
-            for b in (0, 1):
-                if c >= HALF:
-                    look_up(c, b)
-                for r in blocks_of(b):
-                    add_block("v", r, early_acc[r], c)
+                banks = [psum_s.tile([P, T], F32, name="s")]
+                banks += [psum_t.tile([P, T], F32, name="a_t_ps") for i in range(2)]
+                banks += [psum_o.tile([P, T], F32, name="o_ps")]
+            for r, bank in zip(blocks_of(b), banks):
+                sums[r] = bank
+
+        def add_terms(b, c, part=0, parts=1):
+            to_park = c < PARKED_CB[b]
+            first, last = (0, PARKED_CB[b] - 1) if to_park else (PARKED_CB[b], LAST)
+            count = TB // parts
+            for r in blocks_of(b)[part * count : (part + 1) * count]:
+                add_block("v", r, sums[r], c, first, last)
+
+        def park(b):
+            for r in blocks_of(b):
+                parked[r] = held.tile([P, D], F32, name=f"parked{r}")
+                nc.scalar.copy(parked[r][:], sums[r][:])
+
+        open_sums(1)
+        look_up(0, 1)
+        add_terms(1, 0)
+        park(1)
+        for b in (2, 3):
+            open_sums(b)
+            look_up(0, b)
+            add_terms(b, 0)
+        look_up(0, 0)
+        look_up(1, 2)
+        add_terms(2, 1)
+        park(2)
+        open_sums(0)
+        look_up(1, 3)
+        add_terms(3, 1)
+        look_up(1, 0)
+        for c in (0, 1):
+            add_terms(0, c)
+        look_up(1, 1)
+        look_up(2, 3)
+        add_terms(3, 2)
+        park(3)
+        open_sums(1)
+        look_up(2, 0)
+        add_terms(0, 2)
+        add_terms(1, 1)
+        look_up(2, 1)
+        add_terms(1, 2)
+        look_up(2, 2)
+        for b in (0, 1):
+            for part in range(PAIR):
+                look_up(LAST, b, part, PAIR)
+                add_terms(b, LAST, part, PAIR)
         for r in range(EARLY):
-            round_off("v", r, early_acc[r])
+            round_off("v", r, sums[r])
 
         def output(r):
             b, m = divmod(r, CB)
-            acc = psum_acc.tile([P, T], F32, name="acc")
-            for h in range(H):
-                nc.tensor.matmul(
-                    acc[:], weights["o"][:, h, m * P : (m + 1) * P], o[b][:, h, :],
-                    start=(h == 0), stop=(h == H - 1),
+            last = b == B - 1
+            width = T // 2 if r == HEADS - 1 else T
+            for t in range(0, T, width):
+                if last:
+                    acc = psum_s.tile([P, width], F32, name="s")
+                else:
+                    acc = psum_acc.tile([P, width], F32, name="acc")
+                for h in range(H):
+                    nc.tensor.matmul(
+                        acc[:], weights["o"][:, h, m * P : (m + 1) * P], o[b][:, h, t : t + width],
+                        start=(h == 0), stop=(h == H - 1),
+                    )
+                here = slice(b * T + t, b * T + t + width)
+                result = work.tile([P, width], F32, name="result")
+                nc.vector.scalar_tensor_tensor(
+                    result[:], acc[:], type_bo_col[m], x[m][:, here], ADD, ADD
                 )
-            result = work.tile([P, T], F32, name="result")
-            nc.vector.scalar_tensor_tensor(
-                result[:], acc[:], bo_col[m], x[m][:, b * T : (b + 1) * T], ADD, ADD
-            )
-            nc.sync.dma_start(out[m * P : (m + 1) * P, b * T : (b + 1) * T], result[:])
+                nc.sync.dma_start(out[m * P : (m + 1) * P, here], result[:])
 
         def projection(n):
             g, i = divmod(n, TB)
@@ -269,5 +303,5 @@ def tile_enhancedtransformertextclassifier_b_kernel(
             if due(n - 3) and (n - 3) % TB == TB - 1:
                 weigh((n - 3) // TB)
             b, turn = divmod(n, H * TB)
-            if 1 <= b < B - 1 and turn % TB == 0 and HALF + turn // TB < CB:
-                look_up(HALF + turn // TB, b + 1)
+            if 1 <= b < B - 1 and turn == 0:
+                look_up(LAST, b + 1)

@@ -6,8 +6,8 @@ from concourse.masks import make_identity
 F32, BF16, U16 = mybir.dt.float32, mybir.dt.bfloat16, mybir.dt.uint16
 ADD = mybir.AluOpType.add
 MULT = mybir.AluOpType.mult
+MIN = mybir.AluOpType.min
 FUNC = mybir.ActivationFunctionType
-ALONG_FREE = mybir.AxisListType.X
 
 P = 128
 D = 512
@@ -20,6 +20,7 @@ TB = T // P
 PER_COLUMN = 16
 PAIR = 2
 SCALE = 1.0 / math.sqrt(P)
+LARGEST = 3.4e38
 
 HEADS = B * H
 STEPS = HEADS * TB
@@ -43,8 +44,8 @@ def tile_enhancedtransformertextclassifier_b_kernel(
         tc.tile_pool(name="sequences", bufs=3) as sequences,
         tc.tile_pool(name="work", bufs=4) as work,
         tc.tile_pool(name="stat", bufs=6) as stat,
-        tc.psum_pool(name="psum_acc", bufs=2) as psum_acc,
-        tc.psum_pool(name="psum_s", bufs=3) as psum_s,
+        tc.psum_pool(name="psum_acc", bufs=3) as psum_acc,
+        tc.psum_pool(name="psum_s", bufs=2) as psum_s,
         tc.psum_pool(name="psum_t", bufs=2) as psum_t,
         tc.psum_pool(name="psum_o", bufs=1) as psum_o,
     ):
@@ -142,8 +143,8 @@ def tile_enhancedtransformertextclassifier_b_kernel(
 
         def open_sums(b):
             if b % 2 == 0:
-                banks = [psum_acc.tile([P, T], F32, name="acc") for i in range(2)]
-                banks += [psum_s.tile([P, T], F32, name="s") for i in range(2)]
+                banks = [psum_acc.tile([P, T], F32, name="acc") for i in range(3)]
+                banks += [psum_s.tile([P, T], F32, name="s")]
             else:
                 banks = [psum_s.tile([P, T], F32, name="s")]
                 banks += [psum_t.tile([P, T], F32, name="a_t_ps") for i in range(2)]
@@ -201,13 +202,9 @@ def tile_enhancedtransformertextclassifier_b_kernel(
 
         def output(r):
             b, m = divmod(r, CB)
-            last = b == B - 1
             width = T // 2 if r == HEADS - 1 else T
             for t in range(0, T, width):
-                if last:
-                    acc = psum_s.tile([P, width], F32, name="s")
-                else:
-                    acc = psum_acc.tile([P, width], F32, name="acc")
+                acc = psum_acc.tile([P, width], F32, name="acc")
                 for h in range(H):
                     nc.tensor.matmul(
                         acc[:], weights["o"][:, h, m * P : (m + 1) * P], o[b][:, h, t : t + width],
@@ -231,7 +228,7 @@ def tile_enhancedtransformertextclassifier_b_kernel(
             if i == 3 and 0 <= g - LAG_OUT < HEADS:
                 output(g - LAG_OUT)
 
-        s, shift, e, total, a, a_t_ps, a_t = {}, {}, {}, {}, {}, {}, {}
+        s, scaled, shift, e, total, a, a_t_ps, a_t = {}, {}, {}, {}, {}, {}, {}, {}
 
         def scores(n):
             g, i = divmod(n, TB)
@@ -239,16 +236,17 @@ def tile_enhancedtransformertextclassifier_b_kernel(
             nc.tensor.matmul(s[n][:], q[g][:, i * P : (i + 1) * P], k[g][:], start=True, stop=True)
 
         def find_shift(n):
-            top = stat.tile([P, 1], F32, name="top")
-            nc.vector.reduce_max(top[:], s[n][:], axis=ALONG_FREE)
+            scaled[n] = work.tile([P, T], F32, name="scaled")
             shift[n] = stat.tile([P, 1], F32, name="shift")
-            nc.vector.tensor_scalar_mul(shift[n][:], top[:], -SCALE)
+            nc.vector.tensor_scalar(
+                scaled[n][:], s[n][:], -SCALE, LARGEST, MULT, MIN, accum_out=shift[n][:]
+            )
 
         def exponentials(n):
             e[n] = work.tile([P, T], F32, name="e")
             total[n] = stat.tile([P, 1], F32, name="total")
             nc.scalar.activation(
-                e[n][:], s[n][:], FUNC.Exp, bias=shift[n][:], scale=SCALE, accum_out=total[n][:]
+                e[n][:], scaled[n][:], FUNC.Exp, bias=shift[n][:], scale=-1.0, accum_out=total[n][:]
             )
 
         def normalise(n):

@@ -152,12 +152,13 @@ def tile_enhancedtransformertextclassifier_b_kernel(
             for r, bank in zip(blocks_of(b), banks):
                 sums[r] = bank
 
-        def add_terms(b, c, part=0, parts=1):
-            to_park = c < PARKED_CB[b]
+        def add_terms(b, cs, part=0, parts=1):
+            to_park = cs[0] < PARKED_CB[b]
             first, last = (0, PARKED_CB[b] - 1) if to_park else (PARKED_CB[b], LAST)
             count = TB // parts
             for r in blocks_of(b)[part * count : (part + 1) * count]:
-                add_block("v", r, sums[r], c, first, last)
+                for c in cs:
+                    add_block("v", r, sums[r], c, first, last)
 
         def park(b):
             for r in blocks_of(b):
@@ -166,37 +167,35 @@ def tile_enhancedtransformertextclassifier_b_kernel(
 
         open_sums(1)
         look_up(0, 1)
-        add_terms(1, 0)
+        add_terms(1, (0,))
         park(1)
         for b in (2, 3):
             open_sums(b)
             look_up(0, b)
-            add_terms(b, 0)
+            add_terms(b, (0,))
         look_up(0, 0)
         look_up(1, 2)
-        add_terms(2, 1)
+        add_terms(2, (1,))
         park(2)
         open_sums(0)
         look_up(1, 3)
-        add_terms(3, 1)
+        add_terms(3, (1,))
         look_up(1, 0)
-        for c in (0, 1):
-            add_terms(0, c)
+        add_terms(0, (0, 1))
         look_up(1, 1)
         look_up(2, 3)
-        add_terms(3, 2)
+        add_terms(3, (2,))
         park(3)
         open_sums(1)
         look_up(2, 0)
-        add_terms(0, 2)
-        add_terms(1, 1)
+        add_terms(0, (2,))
         look_up(2, 1)
-        add_terms(1, 2)
+        add_terms(1, (1, 2))
         look_up(2, 2)
         for b in (0, 1):
             for part in range(PAIR):
                 look_up(LAST, b, part, PAIR)
-                add_terms(b, LAST, part, PAIR)
+                add_terms(b, (LAST,), part, PAIR)
         for r in range(EARLY):
             round_off("v", r, sums[r])
 

@@ -191,11 +191,11 @@ def tile_enhancedtransformertextclassifier_b_kernel(
         add_terms(0, (2,))
         look_up(2, 1)
         add_terms(1, (1, 2))
-        look_up(2, 2)
         for b in (0, 1):
             for part in range(PAIR):
                 look_up(LAST, b, part, PAIR)
                 add_terms(b, (LAST,), part, PAIR)
+        look_up(2, 2)
         for r in range(EARLY):
             round_off("v", r, sums[r])
 

import math

import concourse.mybir as mybir
from concourse.masks import make_identity

F32, BF16, U16 = mybir.dt.float32, mybir.dt.bfloat16, mybir.dt.uint16
ADD = mybir.AluOpType.add
MULT = mybir.AluOpType.mult
MIN = mybir.AluOpType.min
FUNC = mybir.ActivationFunctionType

P = 128
D = 512
V = 4096
B = 4
T = 512
H = 4
CB = D // P
TB = T // P
PER_COLUMN = 16
PAIR = 2
SCALE = 1.0 / math.sqrt(P)
LARGEST = 3.4e38

HEADS = B * H
STEPS = HEADS * TB

LEAD_QK, LEAD_V, LAG_OUT = 2, 3, 5

EARLY = 8
PARKED_CB = (0, 1, 2, 3)
LAST = CB - 1

FLOPS = 4 * 2 * D * D * B * T + 2 * B * H * 2 * T * T * P


def tile_enhancedtransformertextclassifier_b_kernel(
    tc, tok_emb, pos_emb, type_emb, wq, bq, wk, wv, bv, wo, bo, offs, out
):
    nc = tc.nc
    with (
        tc.tile_pool(name="held", bufs=1) as held,
        tc.tile_pool(name="pairs", bufs=4) as pairs,
        tc.tile_pool(name="sequences", bufs=3) as sequences,
        tc.tile_pool(name="work", bufs=4) as work,
        tc.tile_pool(name="stat", bufs=6) as stat,
        tc.psum_pool(name="psum_acc", bufs=3) as psum_acc,
        tc.psum_pool(name="psum_s", bufs=2) as psum_s,
        tc.psum_pool(name="psum_t", bufs=2) as psum_t,
        tc.psum_pool(name="psum_o", bufs=1) as psum_o,
    ):
        offsets = held.tile([P, B * T // PER_COLUMN], U16, name="offsets")
        nc.sync.dma_start(offsets[:], offs)

        tok = [held.tile([P, V], F32, name=f"tok{c}") for c in range(CB)]
        pos = held.tile([P, CB, T], F32, name="pos")
        weights = {
            name: held.tile([P, CB, D], BF16, name=f"w{name}") for name in ("q", "k", "v", "o")
        }
        rows = held.tile([P, P], F32, name="rows")
        nc.vector.memset(rows[:], 0.0)
        for c in range(CB):
            nc.sync.dma_start(pos[:, c, :], pos_emb[c * P : (c + 1) * P, :])
            nc.sync.dma_start(tok[c][:], tok_emb[c * P : (c + 1) * P, :])
            if c == 0:
                for r, vector in enumerate((type_emb, bq, bv, bo)):
                    nc.sync.dma_start(
                        rows[r * CB : (r + 1) * CB, :], vector.rearrange("(c p) o -> c (p o)", p=P)
                    )
            nc.sync.dma_start(weights["v"][:, c, :], wv[c * P : (c + 1) * P, :])
        for name, w in (("q", wq), ("k", wk), ("o", wo)):
            nc.sync.dma_start(weights[name][:], w.rearrange("(c p) m -> p c m", p=P))

        identity_f = held.tile([P, P], F32, name="identity_f")
        make_identity(nc, identity_f[:])
        acc = psum_acc.tile([P, T], F32, name="acc")
        nc.tensor.transpose(acc[:, 0:P], rows[:], identity_f[:])
        columns = held.tile([P, 4 * CB], F32, name="columns")
        nc.scalar.copy(columns[:], acc[:, 0 : 4 * CB])
        type_col = [columns[:, c : c + 1] for c in range(CB)]
        bq_col = [columns[:, CB + c : CB + c + 1] for c in range(CB)]
        bv_col = [columns[:, 2 * CB + c : 2 * CB + c + 1] for c in range(CB)]
        type_bo = held.tile([P, CB], F32, name="type_bo")
        nc.vector.tensor_tensor(type_bo[:], columns[:, 3 * CB :], columns[:, 0:CB], ADD)
        type_bo_col = [type_bo[:, c : c + 1] for c in range(CB)]

        x = [held.tile([P, B * T], F32, name=f"x{c}") for c in range(CB)]
        x_bf = [held.tile([P, B * T], BF16, name=f"x_bf{c}") for c in range(CB)]

        def look_up(c, b, part=0, parts=1):
            first, count = b * T + part * T // parts, T // parts
            seq = slice(first, first + count)
            piece = offsets[:, first // PER_COLUMN : (first + count) // PER_COLUMN]
            here = pos[:, c, part * count : (part + 1) * count]
            nc.vector.tensor_tensor(x[c][:, seq], tok[c][:].indirect(piece), here, ADD)
            nc.scalar.activation(x_bf[c][:, seq], x[c][:, seq], FUNC.Identity, bias=type_col[c])

        q, k, v_t, o = {}, {}, {}, {}

        def tokens_of(r):
            half, parity = divmod(r, PAIR)
            return slice(half * PAIR * P + parity, (half + 1) * PAIR * P, PAIR)

        def add_block(kind, index, acc, c, first=0, last=CB - 1):
            if kind == "v":
                stationary = x_bf[c][:, tokens_of(index)]
                moving = weights["v"][:, c, :]
            else:
                b, h = divmod(index, H)
                stationary = weights[kind][:, c, h * P : (h + 1) * P]
                moving = x_bf[c][:, b * T : (b + 1) * T]
            nc.tensor.matmul(acc[:], stationary, moving, start=(c == first), stop=(c == last))

        def round_off(kind, index, acc):
            if kind == "q":
                q[index] = pairs.tile([P, T], BF16, name="q")
                nc.scalar.activation(q[index][:], acc[:], FUNC.Identity, bias=bq_col[index % H])
            if kind == "k":
                k[index] = pairs.tile([P, T], BF16, name="k")
                nc.scalar.copy(k[index][:], acc[:])
            if kind == "v":
                b, j = divmod(index, TB)
                if j == 0:
                    v_t[b] = sequences.tile([P, TB, D], BF16, name="v_t")
                if index in parked:
                    nc.vector.tensor_tensor(v_t[b][:, j, :], acc[:], parked[index][:], ADD)
                else:
                    nc.scalar.copy(v_t[b][:, j, :], acc[:])

        def project(kind, index):
            if not 0 <= index < HEADS or (kind == "v" and index < EARLY):
                return
            first = PARKED_CB[index // TB] if kind == "v" else 0
            acc = psum_acc.tile([P, T], F32, name="acc")
            for c in range(first, CB):
                add_block(kind, index, acc, c, first)
            round_off(kind, index, acc)

        sums, parked = {}, {}

        def blocks_of(b):
            return range(b * TB, (b + 1) * TB)

        def open_sums(b):
            if b % 2 == 0:
                banks = [psum_acc.tile([P, T], F32, name="acc") for i in range(3)]
                banks += [psum_s.tile([P, T], F32, name="s")]
            else:
                banks = [psum_s.tile([P, T], F32, name="s")]
                banks += [psum_t.tile([P, T], F32, name="a_t_ps") for i in range(2)]
                banks += [psum_o.tile([P, T], F32, name="o_ps")]
            for r, bank in zip(blocks_of(b), banks):
                sums[r] = bank

        def add_terms(b, cs, part=0, parts=1):
            to_park = cs[0] < PARKED_CB[b]
            first, last = (0, PARKED_CB[b] - 1) if to_park else (PARKED_CB[b], LAST)
            count = TB // parts
            for r in blocks_of(b)[part * count : (part + 1) * count]:
                for c in cs:
                    add_block("v", r, sums[r], c, first, last)

        def park(b):
            for r in blocks_of(b):
                parked[r] = held.tile([P, D], F32, name=f"parked{r}")
                nc.scalar.copy(parked[r][:], sums[r][:])

        open_sums(1)
        look_up(0, 1)
        add_terms(1, (0,))
        park(1)
        for b in (2, 3):
            open_sums(b)
            look_up(0, b)
            add_terms(b, (0,))
        look_up(0, 0)
        look_up(1, 2)
        add_terms(2, (1,))
        park(2)
        open_sums(0)
        look_up(1, 3)
        add_terms(3, (1,))
        look_up(1, 0)
        add_terms(0, (0, 1))
        look_up(1, 1)
        look_up(2, 3)
        add_terms(3, (2,))
        park(3)
        open_sums(1)
        look_up(2, 0)
        add_terms(0, (2,))
        look_up(2, 1)
        add_terms(1, (1, 2))
        for b in (0, 1):
            for part in range(PAIR):
                look_up(LAST, b, part, PAIR)
                add_terms(b, (LAST,), part, PAIR)
        look_up(2, 2)
        for r in range(EARLY):
            round_off("v", r, sums[r])

        def output(r):
            b, m = divmod(r, CB)
            width = T // 2 if r == HEADS - 1 else T
            for t in range(0, T, width):
                acc = psum_acc.tile([P, width], F32, name="acc")
                for h in range(H):
                    nc.tensor.matmul(
                        acc[:], weights["o"][:, h, m * P : (m + 1) * P], o[b][:, h, t : t + width],
                        start=(h == 0), stop=(h == H - 1),
                    )
                here = slice(b * T + t, b * T + t + width)
                result = work.tile([P, width], F32, name="result")
                nc.vector.scalar_tensor_tensor(
                    result[:], acc[:], type_bo_col[m], x[m][:, here], ADD, ADD
                )
                nc.sync.dma_start(out[m * P : (m + 1) * P, here], result[:])

        def projection(n):
            g, i = divmod(n, TB)
            if i == 0:
                project("q", g + LEAD_QK)
            if i == 1:
                project("k", g + LEAD_QK)
            if i == 2:
                project("v", g + LEAD_V)
            if i == 3 and 0 <= g - LAG_OUT < HEADS:
                output(g - LAG_OUT)

        s, scaled, shift, e, total, a, a_t_ps, a_t = {}, {}, {}, {}, {}, {}, {}, {}

        def scores(n):
            g, i = divmod(n, TB)
            s[n] = psum_s.tile([P, T], F32, name="s")
            nc.tensor.matmul(s[n][:], q[g][:, i * P : (i + 1) * P], k[g][:], start=True, stop=True)

        def find_shift(n):
            scaled[n] = work.tile([P, T], F32, name="scaled")
            shift[n] = stat.tile([P, 1], F32, name="shift")
            nc.vector.tensor_scalar(
                scaled[n][:], s[n][:], -SCALE, LARGEST, MULT, MIN, accum_out=shift[n][:]
            )

        def exponentials(n):
            e[n] = work.tile([P, T], F32, name="e")
            total[n] = stat.tile([P, 1], F32, name="total")
            nc.scalar.activation(
                e[n][:], scaled[n][:], FUNC.Exp, bias=shift[n][:], scale=-1.0, accum_out=total[n][:]
            )

        def normalise(n):
            inverse = stat.tile([P, 1], F32, name="inverse")
            nc.vector.reciprocal(inverse[:], total[n][:])
            a[n] = work.tile([P, T], BF16, name="a")
            nc.gpsimd.tensor_scalar(a[n][:], e[n][:], inverse[:], 0.0, MULT, ADD)

        def flip(n):
            a_t_ps[n] = psum_t.tile([P, TB // PAIR, P], F32, name="a_t_ps")
            for half in range(TB // PAIR):
                words = a[n][:, half * PAIR * P : (half + 1) * PAIR * P].bitcast(F32)
                nc.tensor.transpose(a_t_ps[n][:, half, :], words, identity_f[:])

        def keep(n):
            g, i = divmod(n, TB)
            if i == 0:
                a_t[g] = work.tile([P, TB // PAIR, T], F32, name="a_t")
            nc.vector.tensor_copy(a_t[g][:, :, i * P : (i + 1) * P], a_t_ps[n][:])

        def weigh(g):
            b, h = divmod(g, H)
            if h == 0:
                o[b] = sequences.tile([P, H, T], BF16, name="o")
            o_ps = psum_o.tile([P, T], F32, name="o_ps")
            for j in range(TB):
                half, parity = divmod(j, PAIR)
                nc.tensor.matmul(
                    o_ps[:], v_t[b][:, j, h * P : (h + 1) * P],
                    a_t[g][:, half, :].bitcast(BF16)[:, parity::PAIR],
                    start=(j == 0), stop=(j == TB - 1),
                )
            nc.scalar.activation(o[b][:, h, :], o_ps[:], FUNC.Identity, bias=bv_col[h])

        def due(n):
            return 0 <= n < STEPS

        for n in range(-LEAD_V * TB, (HEADS + LAG_OUT) * TB):
            if due(n + 3):
                scores(n + 3)
            if due(n + 2):
                find_shift(n + 2)
            if due(n + 1):
                exponentials(n + 1)
            if due(n):
                normalise(n)
            projection(n)
            if due(n - 1):
                flip(n - 1)
            if due(n - 2):
                keep(n - 2)
            if due(n - 3) and (n - 3) % TB == TB - 1:
                weigh((n - 3) // TB)
            b, turn = divmod(n, H * TB)
            if 1 <= b < B - 1 and turn == 0:
                look_up(LAST, b + 1)
